import numpy as np
import ml_dtypes


def mxq(x, axis, fmt="e4m3"):
    dtype, down = {"e4m3": (ml_dtypes.float8_e4m3fn, 7), "e5m2": (ml_dtypes.float8_e5m2, 14)}[fmt]
    v = np.moveaxis(np.asarray(x, np.float32).astype(ml_dtypes.bfloat16).astype(np.float64), axis, -1)
    blocks = v.reshape(v.shape[:-1] + (-1, 32))
    amax = np.abs(blocks).max(-1, keepdims=True)
    byte = np.maximum(np.where(amax > 0, np.frexp(amax)[1] - 1 + 127, 0) - down, 1)
    scale = np.exp2(byte - 127.0)
    codes = (blocks / scale).astype(np.float32).astype(dtype).astype(np.float64)
    return np.moveaxis((codes * scale).reshape(v.shape), -1, axis)


WIDE = False


def mx_kscale(k):
    if not WIDE:
        return np.ones(k)
    levels = np.array([10, -10, 5, -5, 0])
    a = np.random.permutation(np.resize(levels, k // 512 * 4)).reshape(k // 512, 4)
    idx = np.arange(k)
    return np.exp2(a[idx // 512, idx % 128 // 32])


BF16 = ml_dtypes.bfloat16


def bf(x):
    return np.asarray(x, np.float32).astype(BF16)


def f64(x):
    return np.asarray(x).astype(np.float64)


E2M1 = np.array([0.0, 0.5, 1.0, 1.5, 2.0, 3.0, 4.0, 6.0, -0.0, -0.5, -1.0, -1.5, -2.0, -3.0, -4.0, -6.0])


def pack_weight(w, fmt):
    k, n = w.shape
    w = f64(bf(w)).reshape(k // 32, 32, n)
    amax = np.abs(w).max(1)
    if fmt == "e4m3":
        byte = np.frexp(amax)[1] - 1 + 127 - 7
    else:
        mant, ex = np.frexp(amax / 6.0)
        byte = np.where(mant > 0.5, ex, ex - 1) + 127
    byte = np.clip(np.where(amax > 0, byte, 1), 1, 254)
    scaled = (w * np.exp2(127.0 - byte)[:, None, :]).reshape(k, n).astype(np.float32)
    by_word = np.ascontiguousarray(scaled.reshape(k // 512, 128, 4, n).transpose(0, 1, 3, 2))
    if fmt == "e4m3":
        words = by_word.astype(ml_dtypes.float8_e4m3fn).view(np.uint8)
    else:
        c = by_word.astype(ml_dtypes.float4_e2m1fn).view(np.uint8) & 0xF
        words = c[..., 0::2] | (c[..., 1::2] << 4)
    return np.ascontiguousarray(words), np.ascontiguousarray(byte.astype(np.uint8).reshape(k // 512, 16, n))


def unpack_weight(words, scales, fmt):
    g, p, n, _ = words.shape
    if fmt == "e4m3":
        vals = np.ascontiguousarray(words).view(ml_dtypes.float8_e4m3fn).astype(np.float64)
    else:
        nib = np.empty((g, p, n, 4), np.uint8)
        nib[..., 0::2] = words & 0xF
        nib[..., 1::2] = words >> 4
        vals = E2M1[nib]
    vals = vals * np.repeat(np.exp2(scales.astype(np.float64) - 127.0), 8, axis=1)[..., None]
    return vals.transpose(0, 1, 3, 2).reshape(g * 512, n)


B, D, R, P = 2048, 1024, 128, 3
FMT = "e4m3"
U_NAMES = ("U_0_0", "U_1_0", "U_1_1", "U_2_0", "U_2_1", "U_2_2")


def draw_u(s):
    return pack_weight(np.random.standard_normal((D, R)) / np.sqrt(D) / s[:, None], FMT)


def setup_inputs():
    s = mx_kscale(D)
    out = {"X": bf(np.random.standard_normal((B, D)) * s)}
    for name in U_NAMES:
        words, scales = draw_u(s)
        out[name + "_words"] = words
        out[name + "_scales"] = scales
    out["C"] = bf((1.0 + 0.25 * np.random.standard_normal(P)) / np.sqrt(R))
    out["beta"] = bf(1.0 + 0.25 * np.random.standard_normal(1))
    return out


def reference(X, U_0_0_words, U_0_0_scales, U_1_0_words, U_1_0_scales, U_1_1_words, U_1_1_scales,
              U_2_0_words, U_2_0_scales, U_2_1_words, U_2_1_scales, U_2_2_words, U_2_2_scales, C, beta):
    xq = mxq(f64(X).reshape(B, D), 1, "e4m3")
    c = f64(C)
    u_lists = [[(U_0_0_words, U_0_0_scales)],
               [(U_1_0_words, U_1_0_scales), (U_1_1_words, U_1_1_scales)],
               [(U_2_0_words, U_2_0_scales), (U_2_1_words, U_2_1_scales), (U_2_2_words, U_2_2_scales)]]
    preds = f64(beta)[0]
    for j, u_j in enumerate(u_lists):
        prod = None
        for u_words, u_scales in u_j:
            dot = xq @ unpack_weight(u_words, u_scales, FMT)
            prod = dot if prod is None else prod * dot
        preds = preds + c[j] * np.sum(prod, axis=1)
    return preds

@@ -1,0 +1,195 @@
+from contextlib import ExitStack
+
+import concourse.mybir as mybir
+from concourse.masks import make_identity
+
+F32 = mybir.dt.float32
+BF16 = mybir.dt.bfloat16
+I32 = mybir.dt.int32
+U32 = mybir.dt.uint32
+U8 = mybir.dt.uint8
+FP8X4 = mybir.dt.float8_e4m3fn_x4
+MULT = mybir.AluOpType.mult
+ADD = mybir.AluOpType.add
+COPY = mybir.ActivationFunctionType.Copy
+
+P = 128
+ROWS = 2048
+K = 1024
+RANK = 128
+K_PASS = 4 * P
+PASSES = K // K_PASS
+WORDS_PASS = K_PASS // 2
+TILES = ROWS // P
+ROUND = 2
+ROUNDS = TILES // ROUND
+LAG = 8
+BANK = 512
+LIVE = 4
+
+FLOPS = 2 * ROWS * K * 6 * RANK
+
+
+def tile_polynomialtensorregression_pa_kernel(
+    tc,
+    X,
+    U_0_0_words, U_0_0_scales,
+    U_1_0_words, U_1_0_scales,
+    U_1_1_words, U_1_1_scales,
+    U_2_0_words, U_2_0_scales,
+    U_2_1_words, U_2_1_scales,
+    U_2_2_words, U_2_2_scales,
+    C,
+    beta,
+    out,
+):
+    nc = tc.nc
+    factors = (
+        (U_1_0_words, U_1_0_scales),
+        (U_2_0_words, U_2_0_scales),
+        (U_0_0_words, U_0_0_scales),
+        (U_1_1_words, U_1_1_scales),
+        (U_2_1_words, U_2_1_scales),
+        (U_2_2_words, U_2_2_scales),
+    )
+    width = len(factors) * RANK
+    cols_a = slice(0, BANK)
+    cols_b = slice(BANK, width)
+
+    with ExitStack() as ctx:
+        keep = ctx.enter_context(tc.tile_pool(name="keep", bufs=1))
+        stage = ctx.enter_context(tc.tile_pool(name="stage", bufs=4))
+        psum_t = ctx.enter_context(tc.psum_pool(name="psum_t", bufs=2))
+        psum_d = ctx.enter_context(tc.psum_pool(name="psum_d", bufs=3))
+        ctx.enter_context(tc.manual_schedule())
+
+        x_rows = [keep.tile([P, ROUND, K], BF16, name="x_rows%d" % r) for r in range(ROUNDS)]
+        x_codes = keep.tile([P, TILES, PASSES * P], U32, name="x_codes", align_bytes=64)
+        x_scales = keep.tile([P, TILES, PASSES * P], U8, name="x_scales", align_bytes=64)
+        u_codes = keep.tile([P, PASSES, width], U32, name="u_codes", align_bytes=64)
+        u_scales = keep.tile([P, PASSES, width], U8, name="u_scales", align_bytes=64)
+        ident = keep.tile([P, P], F32, name="ident")
+        warm = keep.tile([P, 1], F32, name="warm")
+        c_bf16 = keep.tile([P, 3], BF16, name="c_bf16")
+        beta_bf16 = keep.tile([P, 1], BF16, name="beta_bf16")
+        c_f32 = keep.tile([P, 3], F32, name="c_f32")
+        beta_f32 = keep.tile([P, 1], F32, name="beta_f32")
+        sum_1 = keep.tile([P, TILES], F32, name="sum_1")
+        sum_2 = keep.tile([P, TILES], F32, name="sum_2")
+        sum_3 = keep.tile([P, TILES], F32, name="sum_3")
+        partial = keep.tile([P, TILES], F32, name="partial")
+        result = keep.tile([P, TILES], F32, name="result")
+
+        nc.vector.memset(u_scales[:].rearrange("p g n -> p (g n)").bitcast(I32), 0)
+        make_identity(nc, ident[:])
+        x_view = X.rearrange("(p j) k -> p j k", j=TILES)
+
+        def load_rows(queue, r):
+            queue.dma_start(out=x_rows[r][:], in_=x_view[:, r * ROUND : (r + 1) * ROUND, :])
+
+        for r in range(2):
+            load_rows(nc.sync, r)
+        for r in range(2, ROUNDS):
+            load_rows(nc.gpsimd, r)
+        for s, (words, scales) in enumerate(factors):
+            cols = slice(s * RANK, (s + 1) * RANK)
+            for quad in range(P // 32):
+                nc.sync.dma_start(
+                    out=u_scales[32 * quad : 32 * quad + LIVE, :, cols].bitcast(I32),
+                    in_=scales[:, LIVE * quad : LIVE * (quad + 1), :]
+                    .rearrange("g r n -> r g n")
+                    .bitcast(I32),
+                )
+        for s, (words, scales) in enumerate(factors):
+            cols = slice(s * RANK, (s + 1) * RANK)
+            nc.sync.dma_start(
+                out=u_codes[:, :, cols].bitcast(I32),
+                in_=words.rearrange("g p n t -> p g (n t)").bitcast(I32),
+            )
+        nc.sync.dma_start(out=c_bf16[:], in_=C.partition_broadcast(P))
+        nc.sync.dma_start(out=beta_bf16[:], in_=beta.partition_broadcast(P))
+        nc.scalar.activation(out=warm[:], in_=ident[:, 0:1], func=COPY)
+
+        def transpose_and_quantise(j):
+            words = x_rows[j // ROUND][:, j % ROUND, :].bitcast(F32)
+            flipped = psum_t.tile([P, PASSES * 2 * P], F32, name="flipped")
+            for g in range(PASSES):
+                for u in range(2):
+                    nc.tensor.transpose(
+                        flipped[:, (2 * g + u) * P : (2 * g + u + 1) * P],
+                        words[:, g * WORDS_PASS + u : (g + 1) * WORDS_PASS : 2],
+                        ident[:],
+                    )
+            grouped = stage.tile([P, PASSES * P * 4], BF16, name="grouped", align_bytes=64)
+            nc.scalar.copy(
+                out=grouped[:].bitcast(F32).rearrange("p (g b u) -> p g b u", g=PASSES, u=2),
+                in_=flipped[:].rearrange("p (g u b) -> p g b u", g=PASSES, u=2),
+            )
+            nc.vector.quantize_mx(
+                out=x_codes[:, j, :].bitcast(FP8X4),
+                scales=x_scales[:, j, :],
+                in_=grouped[:],
+            )
+
+        def multiply(j):
+            dots_a = psum_d.tile([P, BANK], F32, name="dots_a")
+            dots_b = psum_d.tile([P, width - BANK], F32, name="dots_b")
+            for g in range(PASSES):
+                rows = slice(g * P, (g + 1) * P)
+                for dots, cols in ((dots_a, cols_a), (dots_b, cols_b)):
+                    nc.tensor.matmul_mx(
+                        out=dots[:],
+                        lhsT=x_codes[:, j, rows].bitcast(FP8X4),
+                        lhsT_scale=x_scales[:, j, rows],
+                        rhs=u_codes[:, g, cols].bitcast(FP8X4),
+                        rhs_scale=u_scales[:, g, cols],
+                        start=(g == 0),
+                        stop=(g == PASSES - 1),
+                    )
+            return dots_a, dots_b
+
+        def reduce_terms(j, dots_a, dots_b):
+            column = slice(j, j + 1)
+            first = stage.tile([P, 2 * RANK], F32, name="first")
+            unread_s = stage.tile([P, RANK], F32, name="unread_s")
+            unread_v = stage.tile([P, 2 * RANK], F32, name="unread_v")
+            two = stage.tile([P, RANK], F32, name="two")
+            nc.scalar.copy(out=first[:], in_=dots_a[:, 0 : 2 * RANK])
+            nc.scalar.activation(
+                out=unread_s[:], in_=dots_a[:, 2 * RANK : 3 * RANK], func=COPY,
+                accum_out=sum_1[:, column],
+            )
+            nc.vector.scalar_tensor_tensor(
+                out=two[:], in0=first[:, RANK : 2 * RANK], scalar=c_f32[:, 2:3],
+                in1=dots_b[:, 0:RANK], op0=MULT, op1=MULT,
+            )
+            nc.vector.scalar_tensor_tensor(
+                out=unread_v[:, 0:RANK], in0=first[:, 0:RANK], scalar=c_f32[:, 1:2],
+                in1=dots_a[:, 3 * RANK : 4 * RANK], op0=MULT, op1=MULT,
+                accum_out=sum_2[:, column],
+            )
+            nc.vector.scalar_tensor_tensor(
+                out=unread_v[:, RANK : 2 * RANK], in0=two[:], scalar=1.0,
+                in1=dots_b[:, RANK : 2 * RANK], op0=MULT, op1=MULT,
+                accum_out=sum_3[:, column],
+            )
+
+        for r in range(ROUNDS + LAG):
+            if r < ROUNDS:
+                for j in range(r * ROUND, (r + 1) * ROUND):
+                    transpose_and_quantise(j)
+            if r == LAG:
+                nc.vector.tensor_copy(out=c_f32[:], in_=c_bf16[:])
+                nc.vector.tensor_copy(out=beta_f32[:], in_=beta_bf16[:])
+            if r >= LAG:
+                for j in range((r - LAG) * ROUND, (r - LAG + 1) * ROUND):
+                    dots_a, dots_b = multiply(j)
+                    reduce_terms(j, dots_a, dots_b)
+
+        nc.vector.scalar_tensor_tensor(
+            out=partial[:], in0=sum_1[:], scalar=c_f32[:, 0:1], in1=sum_2[:], op0=MULT, op1=ADD
+        )
+        nc.vector.scalar_tensor_tensor(
+            out=result[:], in0=sum_3[:], scalar=beta_f32[:, 0:1], in1=partial[:], op0=ADD, op1=ADD
+        )
+        nc.sync.dma_start(out=out.rearrange("(p j) -> p j", j=TILES), in_=result[:])

@@ -21,10 +21,8 @@ K_PASS = 4 * P
 PASSES = K // K_PASS
 WORDS_PASS = K_PASS // 2
 TILES = ROWS // P
-ROUND = 2
-ROUNDS = TILES // ROUND
-LAG = 8
-BANK = 512
+CHUNK = 2
+CHUNKS = TILES // CHUNK
 LIVE = 4
 
 FLOPS = 2 * ROWS * K * 6 * RANK
@@ -44,74 +42,65 @@ def tile_polynomialtensorregression_pa_kernel(
     out,
 ):
     nc = tc.nc
-    factors = (
-        (U_1_0_words, U_1_0_scales),
-        (U_2_0_words, U_2_0_scales),
-        (U_0_0_words, U_0_0_scales),
-        (U_1_1_words, U_1_1_scales),
-        (U_2_1_words, U_2_1_scales),
-        (U_2_2_words, U_2_2_scales),
+    pairs = (
+        ((U_1_0_words, U_1_0_scales), (U_1_1_words, U_1_1_scales)),
+        ((U_2_0_words, U_2_0_scales), (U_2_1_words, U_2_1_scales)),
+        ((U_2_2_words, U_2_2_scales), (U_0_0_words, U_0_0_scales)),
     )
-    width = len(factors) * RANK
-    cols_a = slice(0, BANK)
-    cols_b = slice(BANK, width)
+    left = slice(0, RANK)
+    right = slice(RANK, 2 * RANK)
 
     with ExitStack() as ctx:
         keep = ctx.enter_context(tc.tile_pool(name="keep", bufs=1))
         stage = ctx.enter_context(tc.tile_pool(name="stage", bufs=4))
-        psum_t = ctx.enter_context(tc.psum_pool(name="psum_t", bufs=2))
-        psum_d = ctx.enter_context(tc.psum_pool(name="psum_d", bufs=3))
+        psum_t = ctx.enter_context(tc.psum_pool(name="psum_t", bufs=3))
+        psum_d = ctx.enter_context(tc.psum_pool(name="psum_d", bufs=5))
         ctx.enter_context(tc.manual_schedule())
 
-        x_rows = [keep.tile([P, ROUND, K], BF16, name="x_rows%d" % r) for r in range(ROUNDS)]
+        x_rows = [keep.tile([P, CHUNK, K], BF16, name="x_rows%d" % c) for c in range(CHUNKS)]
         x_codes = keep.tile([P, TILES, PASSES * P], U32, name="x_codes", align_bytes=64)
         x_scales = keep.tile([P, TILES, PASSES * P], U8, name="x_scales", align_bytes=64)
-        u_codes = keep.tile([P, PASSES, width], U32, name="u_codes", align_bytes=64)
-        u_scales = keep.tile([P, PASSES, width], U8, name="u_scales", align_bytes=64)
+        u_codes = keep.tile([P, len(pairs), PASSES, 2 * RANK], U32, name="u_codes", align_bytes=64)
+        u_scales = keep.tile([P, len(pairs), PASSES, 2 * RANK], U8, name="u_scales", align_bytes=64)
         ident = keep.tile([P, P], F32, name="ident")
         warm = keep.tile([P, 1], F32, name="warm")
         c_bf16 = keep.tile([P, 3], BF16, name="c_bf16")
         beta_bf16 = keep.tile([P, 1], BF16, name="beta_bf16")
         c_f32 = keep.tile([P, 3], F32, name="c_f32")
         beta_f32 = keep.tile([P, 1], F32, name="beta_f32")
+        two = keep.tile([P, TILES, RANK], F32, name="two")
         sum_1 = keep.tile([P, TILES], F32, name="sum_1")
         sum_2 = keep.tile([P, TILES], F32, name="sum_2")
         sum_3 = keep.tile([P, TILES], F32, name="sum_3")
-        partial = keep.tile([P, TILES], F32, name="partial")
+        upto_0 = keep.tile([P, TILES], F32, name="upto_0")
+        upto_1 = keep.tile([P, TILES], F32, name="upto_1")
         result = keep.tile([P, TILES], F32, name="result")
 
-        nc.vector.memset(u_scales[:].rearrange("p g n -> p (g n)").bitcast(I32), 0)
+        nc.vector.memset(u_scales[:].rearrange("p s g n -> p (s g n)").bitcast(I32), 0)
         make_identity(nc, ident[:])
         x_view = X.rearrange("(p j) k -> p j k", j=TILES)
-
-        def load_rows(queue, r):
-            queue.dma_start(out=x_rows[r][:], in_=x_view[:, r * ROUND : (r + 1) * ROUND, :])
-
-        for r in range(2):
-            load_rows(nc.sync, r)
-        for r in range(2, ROUNDS):
-            load_rows(nc.gpsimd, r)
-        for s, (words, scales) in enumerate(factors):
-            cols = slice(s * RANK, (s + 1) * RANK)
-            for quad in range(P // 32):
+        for c in range(CHUNKS):
+            nc.sync.dma_start(out=x_rows[c][:], in_=x_view[:, c * CHUNK : (c + 1) * CHUNK, :])
+        for s, pair in enumerate(pairs):
+            for (words, scales), cols in zip(pair, (left, right)):
                 nc.sync.dma_start(
-                    out=u_scales[32 * quad : 32 * quad + LIVE, :, cols].bitcast(I32),
-                    in_=scales[:, LIVE * quad : LIVE * (quad + 1), :]
-                    .rearrange("g r n -> r g n")
-                    .bitcast(I32),
+                    out=u_codes[:, s, :, cols].bitcast(I32),
+                    in_=words.rearrange("g p n t -> p g (n t)").bitcast(I32),
                 )
-        for s, (words, scales) in enumerate(factors):
-            cols = slice(s * RANK, (s + 1) * RANK)
-            nc.sync.dma_start(
-                out=u_codes[:, :, cols].bitcast(I32),
-                in_=words.rearrange("g p n t -> p g (n t)").bitcast(I32),
-            )
+            for (words, scales), cols in zip(pair, (left, right)):
+                for quad in range(P // 32):
+                    nc.sync.dma_start(
+                        out=u_scales[32 * quad : 32 * quad + LIVE, s, :, cols].bitcast(I32),
+                        in_=scales[:, LIVE * quad : LIVE * (quad + 1), :]
+                        .rearrange("g r n -> r g n")
+                        .bitcast(I32),
+                    )
         nc.sync.dma_start(out=c_bf16[:], in_=C.partition_broadcast(P))
         nc.sync.dma_start(out=beta_bf16[:], in_=beta.partition_broadcast(P))
         nc.scalar.activation(out=warm[:], in_=ident[:, 0:1], func=COPY)
 
         def transpose_and_quantise(j):
-            words = x_rows[j // ROUND][:, j % ROUND, :].bitcast(F32)
+            words = x_rows[j // CHUNK][:, j % CHUNK, :].bitcast(F32)
             flipped = psum_t.tile([P, PASSES * 2 * P], F32, name="flipped")
             for g in range(PASSES):
                 for u in range(2):
@@ -131,65 +120,66 @@ def tile_polynomialtensorregression_pa_kernel(
                 in_=grouped[:],
             )
 
-        def multiply(j):
-            dots_a = psum_d.tile([P, BANK], F32, name="dots_a")
-            dots_b = psum_d.tile([P, width - BANK], F32, name="dots_b")
+        def multiply(j, s):
+            dots = psum_d.tile([P, 2 * RANK], F32, name="dots")
             for g in range(PASSES):
                 rows = slice(g * P, (g + 1) * P)
-                for dots, cols in ((dots_a, cols_a), (dots_b, cols_b)):
-                    nc.tensor.matmul_mx(
-                        out=dots[:],
-                        lhsT=x_codes[:, j, rows].bitcast(FP8X4),
-                        lhsT_scale=x_scales[:, j, rows],
-                        rhs=u_codes[:, g, cols].bitcast(FP8X4),
-                        rhs_scale=u_scales[:, g, cols],
-                        start=(g == 0),
-                        stop=(g == PASSES - 1),
-                    )
-            return dots_a, dots_b
+                nc.tensor.matmul_mx(
+                    out=dots[:],
+                    lhsT=x_codes[:, j, rows].bitcast(FP8X4),
+                    lhsT_scale=x_scales[:, j, rows],
+                    rhs=u_codes[:, s, g, :].bitcast(FP8X4),
+                    rhs_scale=u_scales[:, s, g, :],
+                    start=(g == 0),
+                    stop=(g == PASSES - 1),
+                )
+            return dots
 
-        def reduce_terms(j, dots_a, dots_b):
-            column = slice(j, j + 1)
-            first = stage.tile([P, 2 * RANK], F32, name="first")
+        def to_sbuf(dots):
+            first = stage.tile([P, RANK], F32, name="first")
+            nc.scalar.copy(out=first[:], in_=dots[:, left])
+            return first
+
+        for j in range(TILES):
+            transpose_and_quantise(j)
+
+        for j in range(TILES):
+            dots = multiply(j, 0)
+            first = to_sbuf(dots)
+            unread = stage.tile([P, RANK], F32, name="unread")
+            nc.vector.scalar_tensor_tensor(
+                out=unread[:], in0=first[:], scalar=1.0, in1=dots[:, right], op0=MULT, op1=MULT,
+                accum_out=sum_2[:, j : j + 1],
+            )
+
+        for j in range(TILES):
+            dots = multiply(j, 1)
+            first = to_sbuf(dots)
+            nc.vector.tensor_tensor(out=two[:, j, :], in0=first[:], in1=dots[:, right], op=MULT)
+
+        nc.vector.tensor_copy(out=c_f32[:], in_=c_bf16[:])
+        nc.vector.tensor_copy(out=beta_f32[:], in_=beta_bf16[:])
+        nc.vector.tensor_scalar(
+            out=upto_0[:], in0=sum_2[:], scalar1=c_f32[:, 1:2], scalar2=beta_f32[:, 0:1],
+            op0=MULT, op1=ADD,
+        )
+
+        for j in range(TILES):
+            dots = multiply(j, 2)
+            unread = stage.tile([P, RANK], F32, name="unread")
+            nc.vector.scalar_tensor_tensor(
+                out=unread[:], in0=two[:, j, :], scalar=1.0, in1=dots[:, left], op0=MULT, op1=MULT,
+                accum_out=sum_3[:, j : j + 1],
+            )
             unread_s = stage.tile([P, RANK], F32, name="unread_s")
-            unread_v = stage.tile([P, 2 * RANK], F32, name="unread_v")
-            two = stage.tile([P, RANK], F32, name="two")
-            nc.scalar.copy(out=first[:], in_=dots_a[:, 0 : 2 * RANK])
             nc.scalar.activation(
-                out=unread_s[:], in_=dots_a[:, 2 * RANK : 3 * RANK], func=COPY,
-                accum_out=sum_1[:, column],
+                out=unread_s[:], in_=dots[:, right], func=COPY, accum_out=sum_1[:, j : j + 1]
             )
-            nc.vector.scalar_tensor_tensor(
-                out=two[:], in0=first[:, RANK : 2 * RANK], scalar=c_f32[:, 2:3],
-                in1=dots_b[:, 0:RANK], op0=MULT, op1=MULT,
-            )
-            nc.vector.scalar_tensor_tensor(
-                out=unread_v[:, 0:RANK], in0=first[:, 0:RANK], scalar=c_f32[:, 1:2],
-                in1=dots_a[:, 3 * RANK : 4 * RANK], op0=MULT, op1=MULT,
-                accum_out=sum_2[:, column],
-            )
-            nc.vector.scalar_tensor_tensor(
-                out=unread_v[:, RANK : 2 * RANK], in0=two[:], scalar=1.0,
-                in1=dots_b[:, RANK : 2 * RANK], op0=MULT, op1=MULT,
-                accum_out=sum_3[:, column],
-            )
-
-        for r in range(ROUNDS + LAG):
-            if r < ROUNDS:
-                for j in range(r * ROUND, (r + 1) * ROUND):
-                    transpose_and_quantise(j)
-            if r == LAG:
-                nc.vector.tensor_copy(out=c_f32[:], in_=c_bf16[:])
-                nc.vector.tensor_copy(out=beta_f32[:], in_=beta_bf16[:])
-            if r >= LAG:
-                for j in range((r - LAG) * ROUND, (r - LAG + 1) * ROUND):
-                    dots_a, dots_b = multiply(j)
-                    reduce_terms(j, dots_a, dots_b)
 
         nc.vector.scalar_tensor_tensor(
-            out=partial[:], in0=sum_1[:], scalar=c_f32[:, 0:1], in1=sum_2[:], op0=MULT, op1=ADD
+            out=upto_1[:], in0=sum_1[:], scalar=c_f32[:, 0:1], in1=upto_0[:], op0=MULT, op1=ADD
         )
         nc.vector.scalar_tensor_tensor(
-            out=result[:], in0=sum_3[:], scalar=beta_f32[:, 0:1], in1=partial[:], op0=ADD, op1=ADD
+            out=result[:], in0=sum_3[:], scalar=c_f32[:, 2:3], in1=upto_1[:], op0=MULT, op1=ADD
         )
         nc.sync.dma_start(out=out.rearrange("(p j) -> p j", j=TILES), in_=result[:])

@@ -23,6 +23,7 @@ WORDS_PASS = K_PASS // 2
 TILES = ROWS // P
 CHUNK = 2
 CHUNKS = TILES // CHUNK
+VECTOR_EVERY = 4
 LIVE = 4
 
 FLOPS = 2 * ROWS * K * 6 * RANK
@@ -43,9 +44,9 @@ def tile_polynomialtensorregression_pa_kernel(
 ):
     nc = tc.nc
     pairs = (
-        ((U_1_0_words, U_1_0_scales), (U_1_1_words, U_1_1_scales)),
         ((U_2_0_words, U_2_0_scales), (U_2_1_words, U_2_1_scales)),
         ((U_2_2_words, U_2_2_scales), (U_0_0_words, U_0_0_scales)),
+        ((U_1_0_words, U_1_0_scales), (U_1_1_words, U_1_1_scales)),
     )
     left = slice(0, RANK)
     right = slice(RANK, 2 * RANK)
@@ -99,7 +100,7 @@ def tile_polynomialtensorregression_pa_kernel(
         nc.sync.dma_start(out=beta_bf16[:], in_=beta.partition_broadcast(P))
         nc.scalar.activation(out=warm[:], in_=ident[:, 0:1], func=COPY)
 
-        def transpose_and_quantise(j):
+        def transpose(j):
             words = x_rows[j // CHUNK][:, j % CHUNK, :].bitcast(F32)
             flipped = psum_t.tile([P, PASSES * 2 * P], F32, name="flipped")
             for g in range(PASSES):
@@ -110,10 +111,15 @@ def tile_polynomialtensorregression_pa_kernel(
                         ident[:],
                     )
             grouped = stage.tile([P, PASSES * P * 4], BF16, name="grouped", align_bytes=64)
-            nc.scalar.copy(
-                out=grouped[:].bitcast(F32).rearrange("p (g b u) -> p g b u", g=PASSES, u=2),
-                in_=flipped[:].rearrange("p (g u b) -> p g b u", g=PASSES, u=2),
-            )
+            grouped_words = grouped[:].bitcast(F32).rearrange("p (g b u) -> p g b u", g=PASSES, u=2)
+            flipped_words = flipped[:].rearrange("p (g u b) -> p g b u", g=PASSES, u=2)
+            if j % VECTOR_EVERY == VECTOR_EVERY - 1:
+                nc.vector.tensor_copy(out=grouped_words, in_=flipped_words)
+            else:
+                nc.scalar.copy(out=grouped_words, in_=flipped_words)
+            return grouped
+
+        def quantise(j, grouped):
             nc.vector.quantize_mx(
                 out=x_codes[:, j, :].bitcast(FP8X4),
                 scales=x_scales[:, j, :],
@@ -140,32 +146,20 @@ def tile_polynomialtensorregression_pa_kernel(
             nc.scalar.copy(out=first[:], in_=dots[:, left])
             return first
 
-        for j in range(TILES):
-            transpose_and_quantise(j)
+        waiting = transpose(0)
+        for j in range(1, TILES):
+            grouped = transpose(j)
+            quantise(j - 1, waiting)
+            waiting = grouped
+        quantise(TILES - 1, waiting)
 
         for j in range(TILES):
             dots = multiply(j, 0)
             first = to_sbuf(dots)
-            unread = stage.tile([P, RANK], F32, name="unread")
-            nc.vector.scalar_tensor_tensor(
-                out=unread[:], in0=first[:], scalar=1.0, in1=dots[:, right], op0=MULT, op1=MULT,
-                accum_out=sum_2[:, j : j + 1],
-            )
+            nc.vector.tensor_tensor(out=two[:, j, :], in0=first[:], in1=dots[:, right], op=MULT)
 
         for j in range(TILES):
             dots = multiply(j, 1)
-            first = to_sbuf(dots)
-            nc.vector.tensor_tensor(out=two[:, j, :], in0=first[:], in1=dots[:, right], op=MULT)
-
-        nc.vector.tensor_copy(out=c_f32[:], in_=c_bf16[:])
-        nc.vector.tensor_copy(out=beta_f32[:], in_=beta_bf16[:])
-        nc.vector.tensor_scalar(
-            out=upto_0[:], in0=sum_2[:], scalar1=c_f32[:, 1:2], scalar2=beta_f32[:, 0:1],
-            op0=MULT, op1=ADD,
-        )
-
-        for j in range(TILES):
-            dots = multiply(j, 2)
             unread = stage.tile([P, RANK], F32, name="unread")
             nc.vector.scalar_tensor_tensor(
                 out=unread[:], in0=two[:, j, :], scalar=1.0, in1=dots[:, left], op0=MULT, op1=MULT,
@@ -176,10 +170,26 @@ def tile_polynomialtensorregression_pa_kernel(
                 out=unread_s[:], in_=dots[:, right], func=COPY, accum_out=sum_1[:, j : j + 1]
             )
 
-        nc.vector.scalar_tensor_tensor(
-            out=upto_1[:], in0=sum_1[:], scalar=c_f32[:, 0:1], in1=upto_0[:], op0=MULT, op1=ADD
+        nc.vector.tensor_copy(out=c_f32[:], in_=c_bf16[:])
+        nc.vector.tensor_copy(out=beta_f32[:], in_=beta_bf16[:])
+        nc.vector.tensor_scalar(
+            out=upto_0[:], in0=sum_1[:], scalar1=c_f32[:, 0:1], scalar2=beta_f32[:, 0:1],
+            op0=MULT, op1=ADD,
         )
         nc.vector.scalar_tensor_tensor(
-            out=result[:], in0=sum_3[:], scalar=c_f32[:, 2:3], in1=upto_1[:], op0=MULT, op1=ADD
+            out=upto_1[:], in0=sum_3[:], scalar=c_f32[:, 2:3], in1=upto_0[:], op0=MULT, op1=ADD
+        )
+
+        for j in range(TILES):
+            dots = multiply(j, 2)
+            first = to_sbuf(dots)
+            unread = stage.tile([P, RANK], F32, name="unread")
+            nc.vector.scalar_tensor_tensor(
+                out=unread[:], in0=first[:], scalar=1.0, in1=dots[:, right], op0=MULT, op1=MULT,
+                accum_out=sum_2[:, j : j + 1],
+            )
+
+        nc.vector.scalar_tensor_tensor(
+            out=result[:], in0=sum_2[:], scalar=c_f32[:, 1:2], in1=upto_1[:], op0=MULT, op1=ADD
         )
         nc.sync.dma_start(out=out.rearrange("(p j) -> p j", j=TILES), in_=result[:])

@@ -53,9 +53,7 @@ def tile_polynomialtensorregression_pa_kernel(
 
     with ExitStack() as ctx:
         keep = ctx.enter_context(tc.tile_pool(name="keep", bufs=1))
-        stage = ctx.enter_context(tc.tile_pool(name="stage", bufs=4))
-        psum_t = ctx.enter_context(tc.psum_pool(name="psum_t", bufs=3))
-        psum_d = ctx.enter_context(tc.psum_pool(name="psum_d", bufs=5))
+        stage = ctx.enter_context(tc.tile_pool(name="stage", bufs=8))
         ctx.enter_context(tc.manual_schedule())
 
         x_rows = [keep.tile([P, CHUNK, K], BF16, name="x_rows%d" % c) for c in range(CHUNKS)]
@@ -100,7 +98,7 @@ def tile_polynomialtensorregression_pa_kernel(
         nc.sync.dma_start(out=beta_bf16[:], in_=beta.partition_broadcast(P))
         nc.scalar.activation(out=warm[:], in_=ident[:, 0:1], func=COPY)
 
-        def transpose(j):
+        def transpose(j, psum_t):
             words = x_rows[j // CHUNK][:, j % CHUNK, :].bitcast(F32)
             flipped = psum_t.tile([P, PASSES * 2 * P], F32, name="flipped")
             for g in range(PASSES):
@@ -126,7 +124,7 @@ def tile_polynomialtensorregression_pa_kernel(
                 in_=grouped[:],
             )
 
-        def multiply(j, s):
+        def multiply(j, s, psum_d):
             dots = psum_d.tile([P, 2 * RANK], F32, name="dots")
             for g in range(PASSES):
                 rows = slice(g * P, (g + 1) * P)
@@ -146,20 +144,23 @@ def tile_polynomialtensorregression_pa_kernel(
             nc.scalar.copy(out=first[:], in_=dots[:, left])
             return first
 
-        waiting = transpose(0)
-        for j in range(1, TILES):
-            grouped = transpose(j)
-            quantise(j - 1, waiting)
-            waiting = grouped
-        quantise(TILES - 1, waiting)
+        with tc.psum_pool(name="psum_t", bufs=4) as psum_t:
+            waiting = transpose(0, psum_t)
+            for j in range(1, TILES):
+                grouped = transpose(j, psum_t)
+                quantise(j - 1, waiting)
+                waiting = grouped
+            quantise(TILES - 1, waiting)
+
+        psum_d = ctx.enter_context(tc.psum_pool(name="psum_d", bufs=8, reuse_waits="tile"))
 
         for j in range(TILES):
-            dots = multiply(j, 0)
+            dots = multiply(j, 0, psum_d)
             first = to_sbuf(dots)
             nc.vector.tensor_tensor(out=two[:, j, :], in0=first[:], in1=dots[:, right], op=MULT)
 
         for j in range(TILES):
-            dots = multiply(j, 1)
+            dots = multiply(j, 1, psum_d)
             unread = stage.tile([P, RANK], F32, name="unread")
             nc.vector.scalar_tensor_tensor(
                 out=unread[:], in0=two[:, j, :], scalar=1.0, in1=dots[:, left], op0=MULT, op1=MULT,
@@ -181,7 +182,7 @@ def tile_polynomialtensorregression_pa_kernel(
         )
 
         for j in range(TILES):
-            dots = multiply(j, 2)
+            dots = multiply(j, 2, psum_d)
             first = to_sbuf(dots)
             unread = stage.tile([P, RANK], F32, name="unread")
             nc.vector.scalar_tensor_tensor(

@@ -21,8 +21,9 @@ K_PASS = 4 * P
 PASSES = K // K_PASS
 WORDS_PASS = K_PASS // 2
 TILES = ROWS // P
-CHUNK = 2
-CHUNKS = TILES // CHUNK
+X_LOADS = (1, 1, 2, 4, 4, 2, 1, 1)
+assert sum(X_LOADS) == TILES
+X_LOADS_AHEAD = 3
 VECTOR_EVERY = 4
 LIVE = 4
 
@@ -56,7 +57,7 @@ def tile_polynomialtensorregression_pa_kernel(
         stage = ctx.enter_context(tc.tile_pool(name="stage", bufs=8))
         ctx.enter_context(tc.manual_schedule())
 
-        x_rows = [keep.tile([P, CHUNK, K], BF16, name="x_rows%d" % c) for c in range(CHUNKS)]
+        x_rows = keep.tile([P, TILES, K], BF16, name="x_rows")
         x_codes = keep.tile([P, TILES, PASSES * P], U32, name="x_codes", align_bytes=64)
         x_scales = keep.tile([P, TILES, PASSES * P], U8, name="x_scales", align_bytes=64)
         u_codes = keep.tile([P, len(pairs), PASSES, 2 * RANK], U32, name="u_codes", align_bytes=64)
@@ -78,28 +79,45 @@ def tile_polynomialtensorregression_pa_kernel(
         nc.vector.memset(u_scales[:].rearrange("p s g n -> p (s g n)").bitcast(I32), 0)
         make_identity(nc, ident[:])
         x_view = X.rearrange("(p j) k -> p j k", j=TILES)
-        for c in range(CHUNKS):
-            nc.sync.dma_start(out=x_rows[c][:], in_=x_view[:, c * CHUNK : (c + 1) * CHUNK, :])
-        for s, pair in enumerate(pairs):
-            for (words, scales), cols in zip(pair, (left, right)):
+
+        def load_x(first, last):
+            for n in range(first, last):
+                part = slice(sum(X_LOADS[:n]), sum(X_LOADS[: n + 1]))
+                nc.sync.dma_start(out=x_rows[:, part, :], in_=x_view[:, part, :])
+
+        def load_words(s):
+            for (words, scales), cols in zip(pairs[s], (left, right)):
                 nc.sync.dma_start(
                     out=u_codes[:, s, :, cols].bitcast(I32),
                     in_=words.rearrange("g p n t -> p g (n t)").bitcast(I32),
                 )
-            for (words, scales), cols in zip(pair, (left, right)):
-                for quad in range(P // 32):
-                    nc.sync.dma_start(
-                        out=u_scales[32 * quad : 32 * quad + LIVE, s, :, cols].bitcast(I32),
-                        in_=scales[:, LIVE * quad : LIVE * (quad + 1), :]
-                        .rearrange("g r n -> r g n")
-                        .bitcast(I32),
-                    )
+
+        def load_scales(s, side):
+            words, scales = pairs[s][side]
+            cols = (left, right)[side]
+            for quad in range(P // 32):
+                nc.sync.dma_start(
+                    out=u_scales[32 * quad : 32 * quad + LIVE, s, :, cols].bitcast(I32),
+                    in_=scales[:, LIVE * quad : LIVE * (quad + 1), :]
+                    .rearrange("g r n -> r g n")
+                    .bitcast(I32),
+                )
+
+        load_x(0, X_LOADS_AHEAD)
+        load_words(0)
+        load_scales(0, 0)
+        load_x(X_LOADS_AHEAD, len(X_LOADS))
+        load_scales(0, 1)
+        for s in range(1, len(pairs)):
+            load_words(s)
+            load_scales(s, 0)
+            load_scales(s, 1)
         nc.sync.dma_start(out=c_bf16[:], in_=C.partition_broadcast(P))
         nc.sync.dma_start(out=beta_bf16[:], in_=beta.partition_broadcast(P))
         nc.scalar.activation(out=warm[:], in_=ident[:, 0:1], func=COPY)
 
         def transpose(j, psum_t):
-            words = x_rows[j // CHUNK][:, j % CHUNK, :].bitcast(F32)
+            words = x_rows[:, j, :].bitcast(F32)
             flipped = psum_t.tile([P, PASSES * 2 * P], F32, name="flipped")
             for g in range(PASSES):
                 for u in range(2):

@@ -17,15 +17,18 @@ P = 128
 ROWS = 2048
 K = 1024
 RANK = 128
+ORDERS = 3
 K_PASS = 4 * P
 PASSES = K // K_PASS
 WORDS_PASS = K_PASS // 2
 TILES = ROWS // P
-X_LOADS = (1, 1, 2, 4, 4, 2, 1, 1)
-assert sum(X_LOADS) == TILES
-X_LOADS_AHEAD = 3
-VECTOR_EVERY = 4
+CHUNK = 2
+CHUNKS = TILES // CHUNK
+QUADRANTS = P // 32
 LIVE = 4
+BANKS = 8
+TRANSPOSE_BANKS = 4
+VECTOR_EVERY = 4
 
 FLOPS = 2 * ROWS * K * 6 * RANK
 
@@ -54,19 +57,19 @@ def tile_polynomialtensorregression_pa_kernel(
 
     with ExitStack() as ctx:
         keep = ctx.enter_context(tc.tile_pool(name="keep", bufs=1))
-        stage = ctx.enter_context(tc.tile_pool(name="stage", bufs=8))
+        stage = ctx.enter_context(tc.tile_pool(name="stage", bufs=BANKS))
         ctx.enter_context(tc.manual_schedule())
 
-        x_rows = keep.tile([P, TILES, K], BF16, name="x_rows")
+        x_rows = [keep.tile([P, CHUNK, K], BF16, name="x_rows%d" % c) for c in range(CHUNKS)]
         x_codes = keep.tile([P, TILES, PASSES * P], U32, name="x_codes", align_bytes=64)
         x_scales = keep.tile([P, TILES, PASSES * P], U8, name="x_scales", align_bytes=64)
         u_codes = keep.tile([P, len(pairs), PASSES, 2 * RANK], U32, name="u_codes", align_bytes=64)
         u_scales = keep.tile([P, len(pairs), PASSES, 2 * RANK], U8, name="u_scales", align_bytes=64)
         ident = keep.tile([P, P], F32, name="ident")
         warm = keep.tile([P, 1], F32, name="warm")
-        c_bf16 = keep.tile([P, 3], BF16, name="c_bf16")
+        c_bf16 = keep.tile([P, ORDERS], BF16, name="c_bf16")
         beta_bf16 = keep.tile([P, 1], BF16, name="beta_bf16")
-        c_f32 = keep.tile([P, 3], F32, name="c_f32")
+        c_f32 = keep.tile([P, ORDERS], F32, name="c_f32")
         beta_f32 = keep.tile([P, 1], F32, name="beta_f32")
         two = keep.tile([P, TILES, RANK], F32, name="two")
         sum_1 = keep.tile([P, TILES], F32, name="sum_1")
@@ -80,33 +83,32 @@ def tile_polynomialtensorregression_pa_kernel(
         make_identity(nc, ident[:])
         x_view = X.rearrange("(p j) k -> p j k", j=TILES)
 
-        def load_x(first, last):
-            for n in range(first, last):
-                part = slice(sum(X_LOADS[:n]), sum(X_LOADS[: n + 1]))
-                nc.sync.dma_start(out=x_rows[:, part, :], in_=x_view[:, part, :])
+        def load_x(chunks):
+            for c in chunks:
+                nc.sync.dma_start(out=x_rows[c][:], in_=x_view[:, c * CHUNK : (c + 1) * CHUNK, :])
 
         def load_words(s):
-            for (words, scales), cols in zip(pairs[s], (left, right)):
+            for (u_words, u_bytes), cols in zip(pairs[s], (left, right)):
                 nc.sync.dma_start(
                     out=u_codes[:, s, :, cols].bitcast(I32),
-                    in_=words.rearrange("g p n t -> p g (n t)").bitcast(I32),
+                    in_=u_words.rearrange("g p n t -> p g (n t)").bitcast(I32),
                 )
 
         def load_scales(s, side):
-            words, scales = pairs[s][side]
+            u_words, u_bytes = pairs[s][side]
             cols = (left, right)[side]
-            for quad in range(P // 32):
+            for quad in range(QUADRANTS):
                 nc.sync.dma_start(
                     out=u_scales[32 * quad : 32 * quad + LIVE, s, :, cols].bitcast(I32),
-                    in_=scales[:, LIVE * quad : LIVE * (quad + 1), :]
+                    in_=u_bytes[:, LIVE * quad : LIVE * (quad + 1), :]
                     .rearrange("g r n -> r g n")
                     .bitcast(I32),
                 )
 
-        load_x(0, X_LOADS_AHEAD)
+        load_x(range(0, CHUNKS // 2))
         load_words(0)
         load_scales(0, 0)
-        load_x(X_LOADS_AHEAD, len(X_LOADS))
+        load_x(range(CHUNKS // 2, CHUNKS))
         load_scales(0, 1)
         for s in range(1, len(pairs)):
             load_words(s)
@@ -117,13 +119,13 @@ def tile_polynomialtensorregression_pa_kernel(
         nc.scalar.activation(out=warm[:], in_=ident[:, 0:1], func=COPY)
 
         def transpose(j, psum_t):
-            words = x_rows[:, j, :].bitcast(F32)
+            x_words = x_rows[j // CHUNK][:, j % CHUNK, :].bitcast(F32)
             flipped = psum_t.tile([P, PASSES * 2 * P], F32, name="flipped")
             for g in range(PASSES):
                 for u in range(2):
                     nc.tensor.transpose(
                         flipped[:, (2 * g + u) * P : (2 * g + u + 1) * P],
-                        words[:, g * WORDS_PASS + u : (g + 1) * WORDS_PASS : 2],
+                        x_words[:, g * WORDS_PASS + u : (g + 1) * WORDS_PASS : 2],
                         ident[:],
                     )
             grouped = stage.tile([P, PASSES * P * 4], BF16, name="grouped", align_bytes=64)
@@ -145,11 +147,11 @@ def tile_polynomialtensorregression_pa_kernel(
         def multiply(j, s, psum_d):
             dots = psum_d.tile([P, 2 * RANK], F32, name="dots")
             for g in range(PASSES):
-                rows = slice(g * P, (g + 1) * P)
+                of_pass = slice(g * P, (g + 1) * P)
                 nc.tensor.matmul_mx(
                     out=dots[:],
-                    lhsT=x_codes[:, j, rows].bitcast(FP8X4),
-                    lhsT_scale=x_scales[:, j, rows],
+                    lhsT=x_codes[:, j, of_pass].bitcast(FP8X4),
+                    lhsT_scale=x_scales[:, j, of_pass],
                     rhs=u_codes[:, s, g, :].bitcast(FP8X4),
                     rhs_scale=u_scales[:, s, g, :],
                     start=(g == 0),
@@ -162,7 +164,7 @@ def tile_polynomialtensorregression_pa_kernel(
             nc.scalar.copy(out=first[:], in_=dots[:, left])
             return first
 
-        with tc.psum_pool(name="psum_t", bufs=4) as psum_t:
+        with tc.psum_pool(name="psum_t", bufs=TRANSPOSE_BANKS) as psum_t:
             waiting = transpose(0, psum_t)
             for j in range(1, TILES):
                 grouped = transpose(j, psum_t)
@@ -170,7 +172,7 @@ def tile_polynomialtensorregression_pa_kernel(
                 waiting = grouped
             quantise(TILES - 1, waiting)
 
-        psum_d = ctx.enter_context(tc.psum_pool(name="psum_d", bufs=8, reuse_waits="tile"))
+        psum_d = ctx.enter_context(tc.psum_pool(name="psum_d", bufs=BANKS, reuse_waits="tile"))
 
         for j in range(TILES):
             dots = multiply(j, 0, psum_d)

@@ -24,6 +24,7 @@ WORDS_PASS = K_PASS // 2
 TILES = ROWS // P
 CHUNK = 2
 CHUNKS = TILES // CHUNK
+X_AHEAD = 3
 QUADRANTS = P // 32
 LIVE = 4
 BANKS = 8
@@ -105,11 +106,11 @@ def tile_polynomialtensorregression_pa_kernel(
                     .bitcast(I32),
                 )
 
-        load_x(range(0, CHUNKS // 2))
-        load_words(0)
+        load_x(range(0, X_AHEAD))
         load_scales(0, 0)
-        load_x(range(CHUNKS // 2, CHUNKS))
+        load_x(range(X_AHEAD, CHUNKS))
         load_scales(0, 1)
+        load_words(0)
         for s in range(1, len(pairs)):
             load_words(s)
             load_scales(s, 0)

@@ -106,10 +106,11 @@ def tile_polynomialtensorregression_pa_kernel(
                     .bitcast(I32),
                 )
 
-        load_x(range(0, X_AHEAD))
+        load_x(range(0, 2))
         load_scales(0, 0)
-        load_x(range(X_AHEAD, CHUNKS))
+        load_x(range(2, 4))
         load_scales(0, 1)
+        load_x(range(4, CHUNKS))
         load_words(0)
         for s in range(1, len(pairs)):
             load_words(s)

@@ -22,9 +22,8 @@ K_PASS = 4 * P
 PASSES = K // K_PASS
 WORDS_PASS = K_PASS // 2
 TILES = ROWS // P
-CHUNK = 2
-CHUNKS = TILES // CHUNK
-X_AHEAD = 3
+LOADS = (1, 1, 2, 2, 2, 2, 2, 2, 2)
+X_AHEAD = 4
 QUADRANTS = P // 32
 LIVE = 4
 BANKS = 8
@@ -61,7 +60,8 @@ def tile_polynomialtensorregression_pa_kernel(
         stage = ctx.enter_context(tc.tile_pool(name="stage", bufs=BANKS))
         ctx.enter_context(tc.manual_schedule())
 
-        x_rows = [keep.tile([P, CHUNK, K], BF16, name="x_rows%d" % c) for c in range(CHUNKS)]
+        x_rows = [keep.tile([P, n, K], BF16, name="x_rows%d" % c) for c, n in enumerate(LOADS)]
+        home = [(c, i) for c, n in enumerate(LOADS) for i in range(n)]
         x_codes = keep.tile([P, TILES, PASSES * P], U32, name="x_codes", align_bytes=64)
         x_scales = keep.tile([P, TILES, PASSES * P], U8, name="x_scales", align_bytes=64)
         u_codes = keep.tile([P, len(pairs), PASSES, 2 * RANK], U32, name="u_codes", align_bytes=64)
@@ -86,7 +86,8 @@ def tile_polynomialtensorregression_pa_kernel(
 
         def load_x(chunks):
             for c in chunks:
-                nc.sync.dma_start(out=x_rows[c][:], in_=x_view[:, c * CHUNK : (c + 1) * CHUNK, :])
+                j0 = sum(LOADS[:c])
+                nc.sync.dma_start(out=x_rows[c][:], in_=x_view[:, j0 : j0 + LOADS[c], :])
 
         def load_words(s):
             for (u_words, u_bytes), cols in zip(pairs[s], (left, right)):
@@ -106,11 +107,11 @@ def tile_polynomialtensorregression_pa_kernel(
                     .bitcast(I32),
                 )
 
-        load_x(range(0, 2))
+        load_x(range(0, 3))
         load_scales(0, 0)
-        load_x(range(2, 4))
+        load_x(range(3, 5))
         load_scales(0, 1)
-        load_x(range(4, CHUNKS))
+        load_x(range(5, len(LOADS)))
         load_words(0)
         for s in range(1, len(pairs)):
             load_words(s)
@@ -121,7 +122,7 @@ def tile_polynomialtensorregression_pa_kernel(
         nc.scalar.activation(out=warm[:], in_=ident[:, 0:1], func=COPY)
 
         def transpose(j, psum_t):
-            x_words = x_rows[j // CHUNK][:, j % CHUNK, :].bitcast(F32)
+            x_words = x_rows[home[j][0]][:, home[j][1], :].bitcast(F32)
             flipped = psum_t.tile([P, PASSES * 2 * P], F32, name="flipped")
             for g in range(PASSES):
                 for u in range(2):

@@ -62,10 +62,10 @@ def tile_polynomialtensorregression_pa_kernel(
 
         x_rows = [keep.tile([P, n, K], BF16, name="x_rows%d" % c) for c, n in enumerate(LOADS)]
         home = [(c, i) for c, n in enumerate(LOADS) for i in range(n)]
-        x_codes = keep.tile([P, TILES, PASSES * P], U32, name="x_codes", align_bytes=64)
-        x_scales = keep.tile([P, TILES, PASSES * P], U8, name="x_scales", align_bytes=64)
-        u_codes = keep.tile([P, len(pairs), PASSES, 2 * RANK], U32, name="u_codes", align_bytes=64)
-        u_scales = keep.tile([P, len(pairs), PASSES, 2 * RANK], U8, name="u_scales", align_bytes=64)
+        x_codes = keep.tile([P, TILES, PASSES * P], U32, name="x_codes", align_bytes=256)
+        x_scales = keep.tile([P, TILES, PASSES * P], U8, name="x_scales", align_bytes=256)
+        u_codes = keep.tile([P, len(pairs), PASSES, 2 * RANK], U32, name="u_codes", align_bytes=256)
+        u_scales = keep.tile([P, len(pairs), PASSES, 2 * RANK], U8, name="u_scales", align_bytes=256)
         ident = keep.tile([P, P], F32, name="ident")
         warm = keep.tile([P, 1], F32, name="warm")
         c_bf16 = keep.tile([P, ORDERS], BF16, name="c_bf16")
@@ -131,7 +131,7 @@ def tile_polynomialtensorregression_pa_kernel(
                         x_words[:, g * WORDS_PASS + u : (g + 1) * WORDS_PASS : 2],
                         ident[:],
                     )
-            grouped = stage.tile([P, PASSES * P * 4], BF16, name="grouped", align_bytes=64)
+            grouped = stage.tile([P, PASSES * P * 4], BF16, name="grouped", align_bytes=256)
             grouped_words = grouped[:].bitcast(F32).rearrange("p (g b u) -> p g b u", g=PASSES, u=2)
             flipped_words = flipped[:].rearrange("p (g u b) -> p g b u", g=PASSES, u=2)
             if j % VECTOR_EVERY == VECTOR_EVERY - 1:

@@ -28,6 +28,8 @@ QUADRANTS = P // 32
 LIVE = 4
 BANKS = 8
 TRANSPOSE_BANKS = 4
+PRODUCT_BANKS = BANKS - TRANSPOSE_BANKS
+SORT_FROM = 8
 VECTOR_EVERY = 4
 
 FLOPS = 2 * ROWS * K * 6 * RANK
@@ -49,8 +51,8 @@ def tile_polynomialtensorregression_pa_kernel(
     nc = tc.nc
     pairs = (
         ((U_2_0_words, U_2_0_scales), (U_2_1_words, U_2_1_scales)),
-        ((U_2_2_words, U_2_2_scales), (U_0_0_words, U_0_0_scales)),
-        ((U_1_0_words, U_1_0_scales), (U_1_1_words, U_1_1_scales)),
+        ((U_1_0_words, U_1_0_scales), (U_0_0_words, U_0_0_scales)),
+        ((U_1_1_words, U_1_1_scales), (U_2_2_words, U_2_2_scales)),
     )
     left = slice(0, RANK)
     right = slice(RANK, 2 * RANK)
@@ -64,6 +66,7 @@ def tile_polynomialtensorregression_pa_kernel(
         home = [(c, i) for c, n in enumerate(LOADS) for i in range(n)]
         x_codes = keep.tile([P, TILES, PASSES * P], U32, name="x_codes", align_bytes=256)
         x_scales = keep.tile([P, TILES, PASSES * P], U8, name="x_scales", align_bytes=256)
+        x_sorted = keep.tile([P, TILES - SORT_FROM, 2, K // 4], F32, name="x_sorted")
         u_codes = keep.tile([P, len(pairs), PASSES, 2 * RANK], U32, name="u_codes", align_bytes=256)
         u_scales = keep.tile([P, len(pairs), PASSES, 2 * RANK], U8, name="u_scales", align_bytes=256)
         ident = keep.tile([P, P], F32, name="ident")
@@ -72,16 +75,16 @@ def tile_polynomialtensorregression_pa_kernel(
         beta_bf16 = keep.tile([P, 1], BF16, name="beta_bf16")
         c_f32 = keep.tile([P, ORDERS], F32, name="c_f32")
         beta_f32 = keep.tile([P, 1], F32, name="beta_f32")
-        two = keep.tile([P, TILES, RANK], F32, name="two")
+        factors = keep.tile([P, TILES, 2 * RANK], F32, name="factors")
         sum_1 = keep.tile([P, TILES], F32, name="sum_1")
-        sum_2 = keep.tile([P, TILES], F32, name="sum_2")
-        sum_3 = keep.tile([P, TILES], F32, name="sum_3")
-        upto_0 = keep.tile([P, TILES], F32, name="upto_0")
-        upto_1 = keep.tile([P, TILES], F32, name="upto_1")
+        sum_23 = keep.tile([P, TILES], F32, name="sum_23")
+        order_01 = keep.tile([P, TILES], F32, name="order_01")
         result = keep.tile([P, TILES], F32, name="result")
 
         nc.vector.memset(u_scales[:].rearrange("p s g n -> p (s g n)").bitcast(I32), 0)
         make_identity(nc, ident[:])
+        nc.gpsimd.dma_start(out=c_bf16[:], in_=C.partition_broadcast(P))
+        nc.gpsimd.dma_start(out=beta_bf16[:], in_=beta.partition_broadcast(P))
         x_view = X.rearrange("(p j) k -> p j k", j=TILES)
 
         def load_x(chunks):
@@ -111,30 +114,41 @@ def tile_polynomialtensorregression_pa_kernel(
         load_scales(0, 0)
         load_x(range(3, 5))
         load_scales(0, 1)
-        load_x(range(5, len(LOADS)))
         load_words(0)
+        load_x(range(5, len(LOADS)))
         for s in range(1, len(pairs)):
             load_words(s)
             load_scales(s, 0)
             load_scales(s, 1)
-        nc.sync.dma_start(out=c_bf16[:], in_=C.partition_broadcast(P))
-        nc.sync.dma_start(out=beta_bf16[:], in_=beta.partition_broadcast(P))
         nc.scalar.activation(out=warm[:], in_=ident[:, 0:1], func=COPY)
 
-        def transpose(j, psum_t):
-            x_words = x_rows[home[j][0]][:, home[j][1], :].bitcast(F32)
+        def row_words(j):
+            return x_rows[home[j][0]][:, home[j][1], :].bitcast(F32)
+
+        def sort(j):
+            nc.vector.tensor_copy(
+                out=x_sorted[:, j - SORT_FROM, :, :],
+                in_=row_words(j).rearrange("p (q u) -> p u q", u=2),
+            )
+
+        def transpose(j):
             flipped = psum_t.tile([P, PASSES * 2 * P], F32, name="flipped")
             for g in range(PASSES):
                 for u in range(2):
+                    if j < SORT_FROM:
+                        words = row_words(j)[:, g * WORDS_PASS + u : (g + 1) * WORDS_PASS : 2]
+                    else:
+                        words = x_sorted[:, j - SORT_FROM, u, g * P : (g + 1) * P]
                     nc.tensor.transpose(
-                        flipped[:, (2 * g + u) * P : (2 * g + u + 1) * P],
-                        x_words[:, g * WORDS_PASS + u : (g + 1) * WORDS_PASS : 2],
-                        ident[:],
+                        flipped[:, (2 * g + u) * P : (2 * g + u + 1) * P], words, ident[:]
                     )
+            return flipped
+
+        def group(j, flipped, on_vector=False):
             grouped = stage.tile([P, PASSES * P * 4], BF16, name="grouped", align_bytes=256)
             grouped_words = grouped[:].bitcast(F32).rearrange("p (g b u) -> p g b u", g=PASSES, u=2)
             flipped_words = flipped[:].rearrange("p (g u b) -> p g b u", g=PASSES, u=2)
-            if j % VECTOR_EVERY == VECTOR_EVERY - 1:
+            if on_vector:
                 nc.vector.tensor_copy(out=grouped_words, in_=flipped_words)
             else:
                 nc.scalar.copy(out=grouped_words, in_=flipped_words)
@@ -147,73 +161,119 @@ def tile_polynomialtensorregression_pa_kernel(
                 in_=grouped[:],
             )
 
-        def multiply(j, s, psum_d):
-            dots = psum_d.tile([P, 2 * RANK], F32, name="dots")
-            for g in range(PASSES):
-                of_pass = slice(g * P, (g + 1) * P)
-                nc.tensor.matmul_mx(
-                    out=dots[:],
-                    lhsT=x_codes[:, j, of_pass].bitcast(FP8X4),
-                    lhsT_scale=x_scales[:, j, of_pass],
-                    rhs=u_codes[:, s, g, :].bitcast(FP8X4),
-                    rhs_scale=u_scales[:, s, g, :],
-                    start=(g == 0),
-                    stop=(g == PASSES - 1),
-                )
+        def multiply(j, s, pool, n=2):
+            dots = pool.tile([P, 2, 2 * RANK], F32, name="dots")
+            for i in range(n):
+                for g in range(PASSES):
+                    of_pass = slice(g * P, (g + 1) * P)
+                    nc.tensor.matmul_mx(
+                        out=dots[:, i, :],
+                        lhsT=x_codes[:, j + i, of_pass].bitcast(FP8X4),
+                        lhsT_scale=x_scales[:, j + i, of_pass],
+                        rhs=u_codes[:, s, g, :].bitcast(FP8X4),
+                        rhs_scale=u_scales[:, s, g, :],
+                        start=(g == 0),
+                        stop=(g == PASSES - 1),
+                    )
             return dots
 
         def to_sbuf(dots):
-            first = stage.tile([P, RANK], F32, name="first")
-            nc.scalar.copy(out=first[:], in_=dots[:, left])
+            first = stage.tile([P, 2, RANK], F32, name="first")
+            nc.scalar.copy(out=first[:], in_=dots[:, :, left])
             return first
 
-        with tc.psum_pool(name="psum_t", bufs=TRANSPOSE_BANKS) as psum_t:
-            waiting = transpose(0, psum_t)
-            for j in range(1, TILES):
-                grouped = transpose(j, psum_t)
-                quantise(j - 1, waiting)
-                waiting = grouped
-            quantise(TILES - 1, waiting)
-
-        psum_d = ctx.enter_context(tc.psum_pool(name="psum_d", bufs=BANKS, reuse_waits="tile"))
-
-        for j in range(TILES):
-            dots = multiply(j, 0, psum_d)
-            first = to_sbuf(dots)
-            nc.vector.tensor_tensor(out=two[:, j, :], in0=first[:], in1=dots[:, right], op=MULT)
-
-        for j in range(TILES):
-            dots = multiply(j, 1, psum_d)
-            unread = stage.tile([P, RANK], F32, name="unread")
+        def cube_factor(j, first, dots):
             nc.vector.scalar_tensor_tensor(
-                out=unread[:], in0=two[:, j, :], scalar=1.0, in1=dots[:, left], op0=MULT, op1=MULT,
-                accum_out=sum_3[:, j : j + 1],
-            )
-            unread_s = stage.tile([P, RANK], F32, name="unread_s")
-            nc.scalar.activation(
-                out=unread_s[:], in_=dots[:, right], func=COPY, accum_out=sum_1[:, j : j + 1]
+                out=factors[:, j : j + 2, right], in0=first[:], scalar=c_f32[:, 2:3],
+                in1=dots[:, :, right], op0=MULT, op1=MULT,
             )
 
-        nc.vector.tensor_copy(out=c_f32[:], in_=c_bf16[:])
-        nc.vector.tensor_copy(out=beta_f32[:], in_=beta_bf16[:])
+        def square_factor(j, dots):
+            nc.scalar.activation(
+                out=factors[:, j : j + 2, left], in_=dots[:, :, left], func=COPY, scale=c_f32[:, 1:2]
+            )
+
+        def order_1(j, dots):
+            for i in range(2):
+                unread_s = stage.tile([P, RANK], F32, name="unread_s")
+                nc.scalar.activation(
+                    out=unread_s[:], in_=dots[:, i, right], func=COPY,
+                    accum_out=sum_1[:, j + i : j + i + 1],
+                )
+
+        def orders_23(j, dots, n=2):
+            for i in range(n):
+                unread = stage.tile([P, 2 * RANK], F32, name="unread")
+                nc.vector.scalar_tensor_tensor(
+                    out=unread[:], in0=factors[:, j + i, :], scalar=1.0, in1=dots[:, i, :],
+                    op0=MULT, op1=MULT, accum_out=sum_23[:, j + i : j + i + 1],
+                )
+
+        psum_p = ctx.enter_context(tc.psum_pool(name="psum_p", bufs=PRODUCT_BANKS))
+        with tc.psum_pool(name="psum_t", bufs=TRANSPOSE_BANKS) as psum_t:
+            g = {}
+            d = {}
+            f = {}
+            for j in range(8):
+                g[j] = group(j, transpose(j), j % 3 == 2)
+                if j > 0:
+                    quantise(j - 1, g[j - 1])
+                if j >= 6:
+                    sort(j + 2)
+            quantise(7, g[7])
+            nc.vector.tensor_copy(out=c_f32[:], in_=c_bf16[:])
+            nc.vector.tensor_copy(out=beta_f32[:], in_=beta_bf16[:])
+            sort(10)
+            sort(11)
+            for j in (0, 2, 4):
+                d[j] = multiply(j, 0, psum_p)
+                f[j] = to_sbuf(d[j])
+            for j in range(8, 12):
+                g[j] = group(j, transpose(j))
+            cube_factor(0, f[0], d[0])
+            sort(12)
+            sort(13)
+            quantise(8, g[8])
+            quantise(9, g[9])
+            sort(14)
+            sort(15)
+            d[6] = multiply(6, 0, psum_p)
+            for j in range(12, 16):
+                g[j] = group(j, transpose(j))
+            f[6] = to_sbuf(d[6])
+            quantise(10, g[10])
+            cube_factor(2, f[2], d[2])
+            quantise(11, g[11])
+            quantise(12, g[12])
+            quantise(13, g[13])
+            cube_factor(4, f[4], d[4])
+            quantise(14, g[14])
+            quantise(15, g[15])
+            cube_factor(6, f[6], d[6])
+
+        psum_q = ctx.enter_context(tc.psum_pool(name="psum_q", bufs=TRANSPOSE_BANKS, reuse_waits="tile"))
+        for j in (8, 10):
+            d[j] = multiply(j, 0, psum_q)
+            cube_factor(j, to_sbuf(d[j]), d[j])
+
+        def left_pair(j):
+            e = multiply(j, 1, psum_p)
+            square_factor(j, e)
+            order_1(j, e)
+
+        for j in (12, 14):
+            left_pair(j - 12)
+            d[j] = multiply(j, 0, psum_q)
+            cube_factor(j, to_sbuf(d[j]), d[j])
+        for j in range(4, TILES, 2):
+            left_pair(j)
+            orders_23(j - 4, multiply(j - 4, 2, psum_q))
+        orders_23(12, multiply(12, 2, psum_q))
         nc.vector.tensor_scalar(
-            out=upto_0[:], in0=sum_1[:], scalar1=c_f32[:, 0:1], scalar2=beta_f32[:, 0:1],
+            out=order_01[:], in0=sum_1[:], scalar1=c_f32[:, 0:1], scalar2=beta_f32[:, 0:1],
             op0=MULT, op1=ADD,
         )
-        nc.vector.scalar_tensor_tensor(
-            out=upto_1[:], in0=sum_3[:], scalar=c_f32[:, 2:3], in1=upto_0[:], op0=MULT, op1=ADD
-        )
-
-        for j in range(TILES):
-            dots = multiply(j, 2, psum_d)
-            first = to_sbuf(dots)
-            unread = stage.tile([P, RANK], F32, name="unread")
-            nc.vector.scalar_tensor_tensor(
-                out=unread[:], in0=first[:], scalar=1.0, in1=dots[:, right], op0=MULT, op1=MULT,
-                accum_out=sum_2[:, j : j + 1],
-            )
-
-        nc.vector.scalar_tensor_tensor(
-            out=result[:], in0=sum_2[:], scalar=c_f32[:, 1:2], in1=upto_1[:], op0=MULT, op1=ADD
-        )
+        for j in (14, 15):
+            orders_23(j, multiply(j, 2, psum_q, 1), 1)
+        nc.vector.tensor_tensor(out=result[:], in0=sum_23[:], in1=order_01[:], op=ADD)
         nc.sync.dma_start(out=out.rearrange("(p j) -> p j", j=TILES), in_=result[:])

@@ -83,8 +83,6 @@ def tile_polynomialtensorregression_pa_kernel(
 
         nc.vector.memset(u_scales[:].rearrange("p s g n -> p (s g n)").bitcast(I32), 0)
         make_identity(nc, ident[:])
-        nc.gpsimd.dma_start(out=c_bf16[:], in_=C.partition_broadcast(P))
-        nc.gpsimd.dma_start(out=beta_bf16[:], in_=beta.partition_broadcast(P))
         x_view = X.rearrange("(p j) k -> p j k", j=TILES)
 
         def load_x(chunks):
@@ -116,6 +114,8 @@ def tile_polynomialtensorregression_pa_kernel(
         load_scales(0, 1)
         load_words(0)
         load_x(range(5, len(LOADS)))
+        nc.sync.dma_start(out=c_bf16[:], in_=C.partition_broadcast(P))
+        nc.sync.dma_start(out=beta_bf16[:], in_=beta.partition_broadcast(P))
         for s in range(1, len(pairs)):
             load_words(s)
             load_scales(s, 0)
@@ -221,8 +221,6 @@ def tile_polynomialtensorregression_pa_kernel(
                 if j >= 6:
                     sort(j + 2)
             quantise(7, g[7])
-            nc.vector.tensor_copy(out=c_f32[:], in_=c_bf16[:])
-            nc.vector.tensor_copy(out=beta_f32[:], in_=beta_bf16[:])
             sort(10)
             sort(11)
             for j in (0, 2, 4):
@@ -230,7 +228,6 @@ def tile_polynomialtensorregression_pa_kernel(
                 f[j] = to_sbuf(d[j])
             for j in range(8, 12):
                 g[j] = group(j, transpose(j))
-            cube_factor(0, f[0], d[0])
             sort(12)
             sort(13)
             quantise(8, g[8])
@@ -242,12 +239,15 @@ def tile_polynomialtensorregression_pa_kernel(
                 g[j] = group(j, transpose(j))
             f[6] = to_sbuf(d[6])
             quantise(10, g[10])
-            cube_factor(2, f[2], d[2])
             quantise(11, g[11])
             quantise(12, g[12])
+            nc.vector.tensor_copy(out=c_f32[:], in_=c_bf16[:])
+            nc.vector.tensor_copy(out=beta_f32[:], in_=beta_bf16[:])
+            cube_factor(0, f[0], d[0])
             quantise(13, g[13])
-            cube_factor(4, f[4], d[4])
+            cube_factor(2, f[2], d[2])
             quantise(14, g[14])
+            cube_factor(4, f[4], d[4])
             quantise(15, g[15])
             cube_factor(6, f[6], d[6])
 

@@ -12,6 +12,7 @@ FP8X4 = mybir.dt.float8_e4m3fn_x4
 MULT = mybir.AluOpType.mult
 ADD = mybir.AluOpType.add
 COPY = mybir.ActivationFunctionType.Copy
+IDENTITY = mybir.ActivationFunctionType.Identity
 
 P = 128
 ROWS = 2048
@@ -28,6 +29,7 @@ QUADRANTS = P // 32
 LIVE = 4
 BANKS = 8
 TRANSPOSE_BANKS = 4
+LAST = TILES - 1
 PRODUCT_BANKS = BANKS - TRANSPOSE_BANKS
 SORT_FROM = 8
 VECTOR_EVERY = 4
@@ -75,7 +77,9 @@ def tile_polynomialtensorregression_pa_kernel(
         beta_bf16 = keep.tile([P, 1], BF16, name="beta_bf16")
         c_f32 = keep.tile([P, ORDERS], F32, name="c_f32")
         beta_f32 = keep.tile([P, 1], F32, name="beta_f32")
-        factors = keep.tile([P, TILES, 2 * RANK], F32, name="factors")
+        factors = keep.tile([P, TILES, 2 * RANK + 1], F32, name="factors")
+        one_left = keep.tile([P, P], BF16, name="one_left")
+        one_right = keep.tile([P, 2], BF16, name="one_right")
         sum_1 = keep.tile([P, TILES], F32, name="sum_1")
         sum_23 = keep.tile([P, TILES], F32, name="sum_23")
         order_01 = keep.tile([P, TILES], F32, name="order_01")
@@ -83,6 +87,8 @@ def tile_polynomialtensorregression_pa_kernel(
 
         nc.vector.memset(u_scales[:].rearrange("p s g n -> p (s g n)").bitcast(I32), 0)
         make_identity(nc, ident[:])
+        nc.gpsimd.memset(one_left[:], 1.0 / P)
+        nc.gpsimd.memset(one_right[:], 1.0)
         x_view = X.rearrange("(p j) k -> p j k", j=TILES)
 
         def load_x(chunks):
@@ -163,6 +169,10 @@ def tile_polynomialtensorregression_pa_kernel(
 
         def multiply(j, s, pool, n=2):
             dots = pool.tile([P, 2, 2 * RANK], F32, name="dots")
+            products(j, s, dots, n)
+            return dots
+
+        def products(j, s, dots, n):
             for i in range(n):
                 for g in range(PASSES):
                     of_pass = slice(g * P, (g + 1) * P)
@@ -175,7 +185,6 @@ def tile_polynomialtensorregression_pa_kernel(
                         start=(g == 0),
                         stop=(g == PASSES - 1),
                     )
-            return dots
 
         def to_sbuf(dots):
             first = stage.tile([P, 2, RANK], F32, name="first")
@@ -205,7 +214,7 @@ def tile_polynomialtensorregression_pa_kernel(
             for i in range(n):
                 unread = stage.tile([P, 2 * RANK], F32, name="unread")
                 nc.vector.scalar_tensor_tensor(
-                    out=unread[:], in0=factors[:, j + i, :], scalar=1.0, in1=dots[:, i, :],
+                    out=unread[:], in0=factors[:, j + i, 0 : 2 * RANK], scalar=1.0, in1=dots[:, i, :],
                     op0=MULT, op1=MULT, accum_out=sum_23[:, j + i : j + i + 1],
                 )
 
@@ -265,15 +274,30 @@ def tile_polynomialtensorregression_pa_kernel(
             left_pair(j - 12)
             d[j] = multiply(j, 0, psum_q)
             cube_factor(j, to_sbuf(d[j]), d[j])
-        for j in range(4, TILES, 2):
+        for j in range(4, TILES - 2, 2):
             left_pair(j)
             orders_23(j - 4, multiply(j - 4, 2, psum_q))
-        orders_23(12, multiply(12, 2, psum_q))
-        nc.vector.tensor_scalar(
-            out=order_01[:], in0=sum_1[:], scalar1=c_f32[:, 0:1], scalar2=beta_f32[:, 0:1],
-            op0=MULT, op1=ADD,
+        orders_23(10, multiply(10, 2, psum_q))
+        left_pair(14)
+        nc.scalar.activation(
+            out=order_01[:], in_=sum_1[:], func=IDENTITY, scale=c_f32[:, 0:1], bias=beta_f32[:, 0:1]
         )
-        for j in (14, 15):
+        nc.scalar.activation(
+            out=factors[:, LAST, 2 * RANK : 2 * RANK + 1], in_=sum_1[:, LAST:TILES], func=IDENTITY,
+            scale=c_f32[:, 0:1], bias=beta_f32[:, 0:1],
+        )
+        for j in range(TILES - 4, LAST):
             orders_23(j, multiply(j, 2, psum_q, 1), 1)
-        nc.vector.tensor_tensor(out=result[:], in0=sum_23[:], in1=order_01[:], op=ADD)
+        dots = psum_q.tile([P, 2, 2 * RANK], F32, name="dots")
+        nc.tensor.matmul(dots[:, 1, 0:2], lhsT=one_left[:], rhs=one_right[:], start=True, stop=True)
+        products(LAST, 2, dots, 1)
+        unread_last = stage.tile([P, 2 * RANK + 1], F32, name="unread_last")
+        nc.vector.scalar_tensor_tensor(
+            out=unread_last[:], in0=factors[:, LAST, :], scalar=1.0,
+            in1=dots[:].rearrange("p i n -> p (i n)")[:, 0 : 2 * RANK + 1],
+            op0=MULT, op1=MULT, accum_out=result[:, LAST:TILES],
+        )
+        nc.vector.tensor_tensor(
+            out=result[:, 0:LAST], in0=sum_23[:, 0:LAST], in1=order_01[:, 0:LAST], op=ADD
+        )
         nc.sync.dma_start(out=out.rearrange("(p j) -> p j", j=TILES), in_=result[:])

from contextlib import ExitStack

import concourse.mybir as mybir
from concourse.masks import make_identity

F32 = mybir.dt.float32
BF16 = mybir.dt.bfloat16
I32 = mybir.dt.int32
U32 = mybir.dt.uint32
U8 = mybir.dt.uint8
FP8X4 = mybir.dt.float8_e4m3fn_x4
MULT = mybir.AluOpType.mult
ADD = mybir.AluOpType.add
COPY = mybir.ActivationFunctionType.Copy
IDENTITY = mybir.ActivationFunctionType.Identity

P = 128
ROWS = 2048
K = 1024
RANK = 128
ORDERS = 3
K_PASS = 4 * P
PASSES = K // K_PASS
WORDS_PASS = K_PASS // 2
TILES = ROWS // P
LOADS = (1, 1, 2, 2, 2, 2, 2, 2, 2)
X_AHEAD = 4
QUADRANTS = P // 32
LIVE = 4
BANKS = 8
TRANSPOSE_BANKS = 4
LAST = TILES - 1
PRODUCT_BANKS = BANKS - TRANSPOSE_BANKS
SORT_FROM = 8
VECTOR_EVERY = 4

FLOPS = 2 * ROWS * K * 6 * RANK


def tile_polynomialtensorregression_pa_kernel(
    tc,
    X,
    U_0_0_words, U_0_0_scales,
    U_1_0_words, U_1_0_scales,
    U_1_1_words, U_1_1_scales,
    U_2_0_words, U_2_0_scales,
    U_2_1_words, U_2_1_scales,
    U_2_2_words, U_2_2_scales,
    C,
    beta,
    out,
):
    nc = tc.nc
    pairs = (
        ((U_2_0_words, U_2_0_scales), (U_2_1_words, U_2_1_scales)),
        ((U_1_0_words, U_1_0_scales), (U_0_0_words, U_0_0_scales)),
        ((U_1_1_words, U_1_1_scales), (U_2_2_words, U_2_2_scales)),
    )
    left = slice(0, RANK)
    right = slice(RANK, 2 * RANK)

    with ExitStack() as ctx:
        keep = ctx.enter_context(tc.tile_pool(name="keep", bufs=1))
        stage = ctx.enter_context(tc.tile_pool(name="stage", bufs=BANKS))
        ctx.enter_context(tc.manual_schedule())

        x_rows = [keep.tile([P, n, K], BF16, name="x_rows%d" % c) for c, n in enumerate(LOADS)]
        home = [(c, i) for c, n in enumerate(LOADS) for i in range(n)]
        x_codes = keep.tile([P, TILES, PASSES * P], U32, name="x_codes", align_bytes=256)
        x_scales = keep.tile([P, TILES, PASSES * P], U8, name="x_scales", align_bytes=256)
        x_sorted = keep.tile([P, TILES - SORT_FROM, 2, K // 4], F32, name="x_sorted")
        u_codes = keep.tile([P, len(pairs), PASSES, 2 * RANK], U32, name="u_codes", align_bytes=256)
        u_scales = keep.tile([P, len(pairs), PASSES, 2 * RANK], U8, name="u_scales", align_bytes=256)
        ident = keep.tile([P, P], F32, name="ident")
        warm = keep.tile([P, 1], F32, name="warm")
        c_bf16 = keep.tile([P, ORDERS], BF16, name="c_bf16")
        beta_bf16 = keep.tile([P, 1], BF16, name="beta_bf16")
        c_f32 = keep.tile([P, ORDERS], F32, name="c_f32")
        beta_f32 = keep.tile([P, 1], F32, name="beta_f32")
        factors = keep.tile([P, TILES, 2 * RANK + 1], F32, name="factors")
        one_left = keep.tile([P, P], BF16, name="one_left")
        one_right = keep.tile([P, 2], BF16, name="one_right")
        sum_1 = keep.tile([P, TILES], F32, name="sum_1")
        sum_23 = keep.tile([P, TILES], F32, name="sum_23")
        order_01 = keep.tile([P, TILES], F32, name="order_01")
        result = keep.tile([P, TILES], F32, name="result")

        nc.vector.memset(u_scales[:].rearrange("p s g n -> p (s g n)").bitcast(I32), 0)
        make_identity(nc, ident[:])
        nc.gpsimd.memset(one_left[:], 1.0 / P)
        nc.gpsimd.memset(one_right[:], 1.0)
        x_view = X.rearrange("(p j) k -> p j k", j=TILES)

        def load_x(chunks):
            for c in chunks:
                j0 = sum(LOADS[:c])
                nc.sync.dma_start(out=x_rows[c][:], in_=x_view[:, j0 : j0 + LOADS[c], :])

        def load_words(s):
            for (u_words, u_bytes), cols in zip(pairs[s], (left, right)):
                nc.sync.dma_start(
                    out=u_codes[:, s, :, cols].bitcast(I32),
                    in_=u_words.rearrange("g p n t -> p g (n t)").bitcast(I32),
                )

        def load_scales(s, side):
            u_words, u_bytes = pairs[s][side]
            cols = (left, right)[side]
            for quad in range(QUADRANTS):
                nc.sync.dma_start(
                    out=u_scales[32 * quad : 32 * quad + LIVE, s, :, cols].bitcast(I32),
                    in_=u_bytes[:, LIVE * quad : LIVE * (quad + 1), :]
                    .rearrange("g r n -> r g n")
                    .bitcast(I32),
                )

        load_x(range(0, 3))
        load_scales(0, 0)
        load_x(range(3, 5))
        load_scales(0, 1)
        load_words(0)
        load_x(range(5, len(LOADS)))
        nc.sync.dma_start(out=c_bf16[:], in_=C.partition_broadcast(P))
        nc.sync.dma_start(out=beta_bf16[:], in_=beta.partition_broadcast(P))
        for s in range(1, len(pairs)):
            load_words(s)
            load_scales(s, 0)
            load_scales(s, 1)
        nc.scalar.activation(out=warm[:], in_=ident[:, 0:1], func=COPY)

        def row_words(j):
            return x_rows[home[j][0]][:, home[j][1], :].bitcast(F32)

        def sort(j):
            nc.vector.tensor_copy(
                out=x_sorted[:, j - SORT_FROM, :, :],
                in_=row_words(j).rearrange("p (q u) -> p u q", u=2),
            )

        def transpose(j):
            flipped = psum_t.tile([P, PASSES * 2 * P], F32, name="flipped")
            for g in range(PASSES):
                for u in range(2):
                    if j < SORT_FROM:
                        words = row_words(j)[:, g * WORDS_PASS + u : (g + 1) * WORDS_PASS : 2]
                    else:
                        words = x_sorted[:, j - SORT_FROM, u, g * P : (g + 1) * P]
                    nc.tensor.transpose(
                        flipped[:, (2 * g + u) * P : (2 * g + u + 1) * P], words, ident[:]
                    )
            return flipped

        def group(j, flipped, on_vector=False):
            grouped = stage.tile([P, PASSES * P * 4], BF16, name="grouped", align_bytes=256)
            grouped_words = grouped[:].bitcast(F32).rearrange("p (g b u) -> p g b u", g=PASSES, u=2)
            flipped_words = flipped[:].rearrange("p (g u b) -> p g b u", g=PASSES, u=2)
            if on_vector:
                nc.vector.tensor_copy(out=grouped_words, in_=flipped_words)
            else:
                nc.scalar.copy(out=grouped_words, in_=flipped_words)
            return grouped

        def quantise(j, grouped):
            nc.vector.quantize_mx(
                out=x_codes[:, j, :].bitcast(FP8X4),
                scales=x_scales[:, j, :],
                in_=grouped[:],
            )

        def multiply(j, s, pool, n=2):
            dots = pool.tile([P, 2, 2 * RANK], F32, name="dots")
            products(j, s, dots, n)
            return dots

        def products(j, s, dots, n):
            for i in range(n):
                for g in range(PASSES):
                    of_pass = slice(g * P, (g + 1) * P)
                    nc.tensor.matmul_mx(
                        out=dots[:, i, :],
                        lhsT=x_codes[:, j + i, of_pass].bitcast(FP8X4),
                        lhsT_scale=x_scales[:, j + i, of_pass],
                        rhs=u_codes[:, s, g, :].bitcast(FP8X4),
                        rhs_scale=u_scales[:, s, g, :],
                        start=(g == 0),
                        stop=(g == PASSES - 1),
                    )

        def to_sbuf(dots):
            first = stage.tile([P, 2, RANK], F32, name="first")
            nc.scalar.copy(out=first[:], in_=dots[:, :, left])
            return first

        def cube_factor(j, first, dots):
            nc.vector.scalar_tensor_tensor(
                out=factors[:, j : j + 2, right], in0=first[:], scalar=c_f32[:, 2:3],
                in1=dots[:, :, right], op0=MULT, op1=MULT,
            )

        def square_factor(j, dots):
            nc.scalar.activation(
                out=factors[:, j : j + 2, left], in_=dots[:, :, left], func=COPY, scale=c_f32[:, 1:2]
            )

        def order_1(j, dots):
            for i in range(2):
                unread_s = stage.tile([P, RANK], F32, name="unread_s")
                nc.scalar.activation(
                    out=unread_s[:], in_=dots[:, i, right], func=COPY,
                    accum_out=sum_1[:, j + i : j + i + 1],
                )

        def orders_23(j, dots, n=2):
            for i in range(n):
                unread = stage.tile([P, 2 * RANK], F32, name="unread")
                nc.vector.scalar_tensor_tensor(
                    out=unread[:], in0=factors[:, j + i, 0 : 2 * RANK], scalar=1.0, in1=dots[:, i, :],
                    op0=MULT, op1=MULT, accum_out=sum_23[:, j + i : j + i + 1],
                )

        psum_p = ctx.enter_context(tc.psum_pool(name="psum_p", bufs=PRODUCT_BANKS))
        with tc.psum_pool(name="psum_t", bufs=TRANSPOSE_BANKS) as psum_t:
            g = {}
            d = {}
            f = {}
            for j in range(8):
                g[j] = group(j, transpose(j), j % 3 == 2)
                if j > 0:
                    quantise(j - 1, g[j - 1])
                if j >= 6:
                    sort(j + 2)
            quantise(7, g[7])
            sort(10)
            sort(11)
            for j in (0, 2, 4):
                d[j] = multiply(j, 0, psum_p)
                f[j] = to_sbuf(d[j])
            for j in range(8, 12):
                g[j] = group(j, transpose(j))
            sort(12)
            sort(13)
            quantise(8, g[8])
            quantise(9, g[9])
            sort(14)
            sort(15)
            d[6] = multiply(6, 0, psum_p)
            for j in range(12, 16):
                g[j] = group(j, transpose(j))
            f[6] = to_sbuf(d[6])
            quantise(10, g[10])
            quantise(11, g[11])
            quantise(12, g[12])
            nc.vector.tensor_copy(out=c_f32[:], in_=c_bf16[:])
            nc.vector.tensor_copy(out=beta_f32[:], in_=beta_bf16[:])
            cube_factor(0, f[0], d[0])
            quantise(13, g[13])
            cube_factor(2, f[2], d[2])
            quantise(14, g[14])
            cube_factor(4, f[4], d[4])
            quantise(15, g[15])
            cube_factor(6, f[6], d[6])

        psum_q = ctx.enter_context(tc.psum_pool(name="psum_q", bufs=TRANSPOSE_BANKS, reuse_waits="tile"))
        for j in (8, 10):
            d[j] = multiply(j, 0, psum_q)
            cube_factor(j, to_sbuf(d[j]), d[j])

        def left_pair(j):
            e = multiply(j, 1, psum_p)
            square_factor(j, e)
            order_1(j, e)

        for j in (12, 14):
            left_pair(j - 12)
            d[j] = multiply(j, 0, psum_q)
            cube_factor(j, to_sbuf(d[j]), d[j])
        for j in range(4, TILES - 2, 2):
            left_pair(j)
            orders_23(j - 4, multiply(j - 4, 2, psum_q))
        orders_23(10, multiply(10, 2, psum_q))
        left_pair(14)
        nc.scalar.activation(
            out=order_01[:], in_=sum_1[:], func=IDENTITY, scale=c_f32[:, 0:1], bias=beta_f32[:, 0:1]
        )
        nc.scalar.activation(
            out=factors[:, LAST, 2 * RANK : 2 * RANK + 1], in_=sum_1[:, LAST:TILES], func=IDENTITY,
            scale=c_f32[:, 0:1], bias=beta_f32[:, 0:1],
        )
        for j in range(TILES - 4, LAST):
            orders_23(j, multiply(j, 2, psum_q, 1), 1)
        dots = psum_q.tile([P, 2, 2 * RANK], F32, name="dots")
        nc.tensor.matmul(dots[:, 1, 0:2], lhsT=one_left[:], rhs=one_right[:], start=True, stop=True)
        products(LAST, 2, dots, 1)
        unread_last = stage.tile([P, 2 * RANK + 1], F32, name="unread_last")
        nc.vector.scalar_tensor_tensor(
            out=unread_last[:], in0=factors[:, LAST, :], scalar=1.0,
            in1=dots[:].rearrange("p i n -> p (i n)")[:, 0 : 2 * RANK + 1],
            op0=MULT, op1=MULT, accum_out=result[:, LAST:TILES],
        )
        nc.vector.tensor_tensor(
            out=result[:, 0:LAST], in0=sum_23[:, 0:LAST], in1=order_01[:, 0:LAST], op=ADD
        )
        nc.sync.dma_start(out=out.rearrange("(p j) -> p j", j=TILES), in_=result[:])
